import numpy as np
import ml_dtypes


def mxq(x, axis, fmt="e4m3"):
    dtype, down = {"e4m3": (ml_dtypes.float8_e4m3fn, 7), "e5m2": (ml_dtypes.float8_e5m2, 14)}[fmt]
    v = np.moveaxis(np.asarray(x, np.float32).astype(ml_dtypes.bfloat16).astype(np.float64), axis, -1)
    blocks = v.reshape(v.shape[:-1] + (-1, 32))
    amax = np.abs(blocks).max(-1, keepdims=True)
    byte = np.maximum(np.where(amax > 0, np.frexp(amax)[1] - 1 + 127, 0) - down, 1)
    scale = np.exp2(byte - 127.0)
    codes = (blocks / scale).astype(np.float32).astype(dtype).astype(np.float64)
    return np.moveaxis((codes * scale).reshape(v.shape), -1, axis)


WIDE = False


def mx_kscale(k):
    if not WIDE:
        return np.ones(k)
    levels = np.array([10, -10, 5, -5, 0])
    a = np.random.permutation(np.resize(levels, k // 512 * 4)).reshape(k // 512, 4)
    idx = np.arange(k)
    return np.exp2(a[idx // 512, idx % 128 // 32])


BF16 = ml_dtypes.bfloat16


def bf(x):
    return np.asarray(x, np.float32).astype(BF16)


def f64(x):
    return np.asarray(x).astype(np.float64)


N, I0, O0, I1, O1, I2, O2, D0, D1, D2 = 1024, 512, 512, 256, 256, 128, 128, 1, 3, 5


def irrep_linear(x, w):
    return (x.transpose(2, 0, 1) @ w.transpose(2, 1, 0)).transpose(1, 2, 0)


def setup_inputs():
    s = mx_kscale(I0)
    return {"x0e": bf(np.random.standard_normal((N, I0, D0)) * s[None, :, None]),
            "x1o": bf(np.random.standard_normal((N, I1, D1))),
            "x2e": bf(np.random.standard_normal((N, I2, D2))),
            "w0e": bf(np.random.standard_normal((O0, I0, D0)) / np.sqrt(I0) / s[None, :, None]),
            "w1o": bf(np.random.standard_normal((O1, I1, D1)) / np.sqrt(I1)),
            "w2e": bf(np.random.standard_normal((O2, I2, D2)) / np.sqrt(I2)),
            "bias": bf(np.random.standard_normal(O0) * 0.5)}


def reference(x0e, x1o, x2e, w0e, w1o, w2e, bias):
    y0e = irrep_linear(mxq(f64(x0e), 1, "e4m3"), mxq(f64(w0e), 1, "e4m3")) + f64(bias)[None, :, None]
    y1o = irrep_linear(f64(x1o), f64(w1o))
    y2e = irrep_linear(f64(x2e), f64(w2e))
    n = x0e.shape[0]
    return np.concatenate([y0e.reshape(n, -1), y1o.reshape(n, -1), y2e.reshape(n, -1)], axis=-1)

@@ -1,0 +1,277 @@
+from contextlib import ExitStack
+
+import concourse.mybir as mybir
+from concourse.masks import make_identity
+
+FLOPS = 2 * 1024 * (512 * 512 + 3 * 256 * 256 + 5 * 128 * 128)
+
+BF16 = mybir.dt.bfloat16
+F32 = mybir.dt.float32
+U32 = mybir.dt.uint32
+U8 = mybir.dt.uint8
+FP8X4 = mybir.dt.float8_e4m3fn_x4
+ADD = mybir.AluOpType.add
+MULT = mybir.AluOpType.mult
+
+P = 128
+NT = 8
+MANUAL = True
+CHUNKS = ((0, 2), (2, 4), (4, 8))
+
+
+def tile_linearlayer_kernel(tc, x0e, x1o, x2e, w0e, w1o, w2e, bias, out):
+    nc = tc.nc
+    with ExitStack() as ctx:
+        if MANUAL:
+            ctx.enter_context(tc.manual_schedule())
+        keep = ctx.enter_context(tc.tile_pool(name="keep", bufs=1))
+        tp = ctx.enter_context(tc.psum_pool(name="tp", bufs=3))
+        acc = ctx.enter_context(tc.psum_pool(name="acc", bufs=5))
+
+        x0v = x0e.rearrange("(p t) i d -> p t (i d)", t=NT)
+        x1v = x1o.rearrange("(p t) i d -> p t (i d)", t=NT)
+        x2v = x2e.rearrange("(p t) i d -> p t (i d)", t=NT)
+        outv = out.rearrange("(p t) c -> p t c", t=NT)
+
+        def evac(eng, dst, src):
+            if eng == "v":
+                nc.vector.tensor_copy(out=dst, in_=src)
+            else:
+                nc.scalar.copy(out=dst, in_=src)
+
+        ident_f = keep.tile([P, P], F32, name="ident_f")
+        make_identity(nc, ident_f[:])
+        ident_b = keep.tile([P, P], BF16, name="ident_b")
+        make_identity(nc, ident_b[:])
+        ones = keep.tile([P, P], BF16, name="ones")
+        nc.vector.memset(ones[:], 1.0)
+        brow = keep.tile([P, 512], BF16, name="brow")
+        nc.vector.memset(brow[:], 0.0)
+
+        where = {}
+        x_sb = {}
+
+        def load_x(kind, c):
+            view, width = {0: (x0v, 512), 1: (x1v, 768), 2: (x2v, 640)}[kind]
+            lo, hi = CHUNKS[c]
+            a = keep.tile([P, (hi - lo) * width], BF16, name="x%d_sb%d" % (kind, c))
+            nc.sync.dma_start(out=a[:].rearrange("p (t c) -> p t c", t=hi - lo), in_=view[:, lo:hi, :])
+            x_sb[(kind, c)] = a
+
+        for c, (lo, hi) in enumerate(CHUNKS):
+            for t in range(lo, hi):
+                where[t] = (c, t - lo, hi - lo)
+
+        w1_sb = keep.tile([P, 2 * 768], BF16, name="w1_sb")
+        nc.sync.dma_start(
+            out=w1_sb[:].rearrange("p (a c) -> p a c", a=2),
+            in_=w1o.rearrange("(a p) i d -> p a (i d)", p=P),
+        )
+        load_x(1, 0)
+        nc.sync.dma_start(out=brow[0:1, :], in_=bias.rearrange("(a o) -> a o", a=1))
+        w0_sb = keep.tile([P, 4 * 512], BF16, name="w0_sb")
+        nc.sync.dma_start(
+            out=w0_sb[:].rearrange("p (a c) -> p a c", a=4),
+            in_=w0e.rearrange("(a p) i d -> p a (i d)", p=P),
+        )
+        load_x(0, 0)
+        w2_sb = keep.tile([P, 640], BF16, name="w2_sb")
+        nc.sync.dma_start(out=w2_sb[:], in_=w2e.rearrange("o i d -> o (i d)"))
+        load_x(2, 0)
+        load_x(1, 1)
+        load_x(2, 1)
+        load_x(0, 1)
+        load_x(2, 2)
+        load_x(1, 2)
+        load_x(0, 2)
+
+        bias_bc = keep.tile([P, 512], F32, name="bias_bc")
+
+        def prep_bias():
+            pb = acc.tile([P, 512], F32, name="pb", tag="acc")
+            nc.tensor.matmul(out=pb[:], lhsT=ones[:], rhs=brow[:], start=True, stop=True)
+            evac("v", bias_bc[:], pb[:])
+
+        w2d = keep.tile([P, 640], BF16, name="w2d")
+        w2T = keep.tile([P, 5, P], BF16, name="w2T")
+
+        def sort_w2():
+            nc.gpsimd.tensor_scalar(
+                out=w2d[:].rearrange("p (m i) -> p m i", m=5),
+                in0=w2_sb[:].rearrange("p (i m) -> p m i", m=5),
+                scalar1=1.0, scalar2=0.0, op0=MULT, op1=ADD,
+            )
+
+        def prep_w2():
+            bk = tp.tile([P, 5, P], BF16, name="bk_w2", tag="tp")
+            for m in range(5):
+                nc.tensor.transpose(bk[:, m, :], w2d[:, m * P : (m + 1) * P], ident_b[:])
+            evac("s", w2T[:], bk[:])
+
+        w1Tb = []
+
+        def prep_w1():
+            w1w = w1_sb[:].bitcast(F32).rearrange("p (a j r) -> p a j r", a=2, r=3)
+            for a in range(2):
+                bk = tp.tile([P, 3, P], F32, name="bk_w1", tag="tp")
+                for r in range(3):
+                    nc.tensor.transpose(bk[:, r, :], w1w[:, a, :, r], ident_f[:])
+                wt = keep.tile([P, 3 * P], F32, name="w1T%d" % a)
+                evac("sv"[a], wt[:].rearrange("p (r o) -> p r o", r=3), bk[:])
+                w1Tb.append(wt[:].bitcast(BF16).rearrange("p (r o e) -> p r o e", r=3, e=2))
+
+        gw = keep.tile([P, 2048], BF16, name="gw", align_bytes=64)
+        wq = keep.tile([P, 512], U32, name="wq", align_bytes=64)
+        ws = keep.tile([P, 512], U8, name="ws", align_bytes=64)
+
+        def prep_w0():
+            w0f = w0_sb[:].bitcast(F32)
+            gwf = gw[:].bitcast(F32).rearrange("p (o u) -> p o u", u=2)
+            for b in range(2):
+                bk = tp.tile([P, 2, 256], F32, name="bk_w0", tag="tp")
+                for aa in range(2):
+                    for u in range(2):
+                        c0 = 256 * (2 * b + aa) + 128 * u
+                        nc.tensor.transpose(bk[:, u, aa * P : (aa + 1) * P], w0f[:, c0 : c0 + P], ident_f[:])
+                evac("vs"[b], gwf[:, 256 * b : 256 * b + 256, :], bk[:].rearrange("p u o -> p o u"))
+
+        def quant_w0():
+            nc.vector.quantize_mx(out=wq[:].bitcast(FP8X4), scales=ws[:], in_=gw[:])
+
+        gx = {}
+        xq = {}
+        xs = {}
+        x1Tb = {}
+        x2T = {}
+        x2d = {}
+
+        def sort2(g):
+            c, k, n = where[2 * g]
+            d = keep.tile([P, 2 * 640], BF16, name="x2d%d" % g)
+            nc.gpsimd.tensor_scalar(
+                out=d[:].rearrange("p (t m i) -> p t m i", t=2, m=5),
+                in0=x_sb[(2, c)][:, 640 * k : 640 * (k + 2)].rearrange("p (t i m) -> p t m i", t=2, m=5),
+                scalar1=1.0, scalar2=0.0, op0=MULT, op1=ADD,
+            )
+            x2d[g] = d
+
+        def flip0(g):
+            c, k, n = where[2 * g]
+            xf = x_sb[(0, c)][:].bitcast(F32)
+            bk0 = tp.tile([P, 2, 256], F32, name="bk_x0", tag="tp")
+            for tt in range(2):
+                for u in range(2):
+                    c0 = 256 * (k + tt) + 128 * u
+                    nc.tensor.transpose(bk0[:, u, tt * P : (tt + 1) * P], xf[:, c0 : c0 + P], ident_f[:])
+            a = keep.tile([P, 1024], BF16, name="gx%d" % g, align_bytes=64)
+            evac("v", a[:].bitcast(F32).rearrange("p (n u) -> p n u", u=2), bk0[:].rearrange("p u n -> p n u"))
+            gx[g] = a
+
+        def quant0(g):
+            q = keep.tile([P, 256], U32, name="xq%d" % g, align_bytes=64)
+            s = keep.tile([P, 256], U8, name="xs%d" % g, align_bytes=64)
+            nc.vector.quantize_mx(out=q[:].bitcast(FP8X4), scales=s[:], in_=gx[g][:])
+            xq[g] = q
+            xs[g] = s
+
+        def flip1(t):
+            c, k, n = where[t]
+            xw = x_sb[(1, c)][:].bitcast(F32).rearrange("p (t j r) -> p t j r", t=n, r=3)
+            bk1 = tp.tile([P, 3, P], F32, name="bk_x1", tag="tp")
+            for r in range(3):
+                nc.tensor.transpose(bk1[:, r, :], xw[:, k, :, r], ident_f[:])
+            xt = keep.tile([P, 3 * P], F32, name="x1T%d" % t)
+            evac("s", xt[:].rearrange("p (r n) -> p r n", r=3), bk1[:])
+            x1Tb[t] = xt[:].bitcast(BF16).rearrange("p (r n e) -> p r n e", r=3, e=2)
+
+        def flip2(t):
+            g, tt = divmod(t, 2)
+            bk2 = tp.tile([P, 5, P], BF16, name="bk_x2", tag="tp")
+            for m in range(5):
+                c0 = 640 * tt + 128 * m
+                nc.tensor.transpose(bk2[:, m, :], x2d[g][:, c0 : c0 + P], ident_b[:])
+            x2t = keep.tile([P, 5, P], BF16, name="x2T%d" % t)
+            evac("s", x2t[:], bk2[:])
+            x2T[t] = x2t
+
+        o_sbs = {}
+
+        def o_of(t):
+            if t not in o_sbs:
+                o_sbs[t] = keep.tile([P, 1920], F32, name="o_sb%d" % t)
+            return o_sbs[t]
+
+        def mm1(t, h):
+            o_sb = o_of(t)
+            py = acc.tile([P, 3, P], F32, name="py1", tag="acc")
+            for m in range(3):
+                for par in range(2):
+                    r, e = divmod(3 * par + m, 2)
+                    nc.tensor.matmul(
+                        out=py[:, m, :], lhsT=x1Tb[t][:, r, :, e], rhs=w1Tb[h][:, r, :, e],
+                        start=(par == 0), stop=(par == 1),
+                    )
+            c0 = 512 + 384 * h
+            eng = "s" if (h == 1 and t % 2 == 0) else "v"
+            evac(eng, o_sb[:, c0 : c0 + 384].rearrange("p (o m) -> p o m", m=3), py[:].rearrange("p m o -> p o m"))
+
+        def mm0(t):
+            o_sb = o_of(t)
+            g, tt = divmod(t, 2)
+            p0 = acc.tile([P, 512], F32, name="p0", tag="acc")
+            nc.tensor.matmul_mx(
+                out=p0[:],
+                lhsT=xq[g][:, tt * P : (tt + 1) * P].bitcast(FP8X4), lhsT_scale=xs[g][:, tt * P : (tt + 1) * P],
+                rhs=wq[:].bitcast(FP8X4), rhs_scale=ws[:],
+                start=True, stop=True,
+            )
+            nc.vector.tensor_tensor(out=o_sb[:, 0:512], in0=p0[:], in1=bias_bc[:], op=ADD)
+
+        def mm2(t, h):
+            o_sb = o_of(t)
+            py = acc.tile([P, 5, 64], F32, name="py2", tag="acc")
+            for m in range(5):
+                nc.tensor.matmul(
+                    out=py[:, m, :], lhsT=x2T[t][:, m, :], rhs=w2T[:, m, 64 * h : 64 * h + 64],
+                    start=True, stop=True,
+                )
+            c0 = 1280 + 320 * h
+            eng = "v" if (t == NT - 1 and h == 0) else "s"
+            evac(eng, o_sb[:, c0 : c0 + 320].rearrange("p (o m) -> p o m", m=5), py[:].rearrange("p m o -> p o m"))
+
+        sort_w2()
+        for g in range(NT // 2):
+            sort2(g)
+
+        prep_w1()
+        flip1(0)
+        flip1(1)
+        prep_bias()
+        prep_w0()
+        flip0(0)
+        quant_w0()
+        prep_w2()
+        quant0(0)
+        flip2(0)
+        flip2(1)
+        for t in range(NT):
+            nxt = t + 2
+            if nxt < NT:
+                flip1(nxt)
+            mm1(t, 0)
+            mm0(t)
+            mm1(t, 1)
+            if t == NT - 1:
+                nc.sync.dma_start(out=outv[:, t, 0:1280], in_=o_of(t)[:, 0:1280])
+            if nxt < NT and t % 2 == 0:
+                flip0(nxt // 2)
+            if nxt < NT:
+                flip2(nxt)
+            mm2(t, 0)
+            mm2(t, 1)
+            if nxt < NT and t % 2 == 0:
+                quant0(nxt // 2)
+            if t == NT - 1:
+                nc.sync.dma_start(out=outv[:, t, 1280:1920], in_=o_of(t)[:, 1280:1920])
+            else:
+                nc.sync.dma_start(out=outv[:, t, :], in_=o_of(t)[:])

@@ -110,15 +110,14 @@ def tile_linearlayer_kernel(tc, x0e, x1o, x2e, w0e, w1o, w2e, bias, out):
 
         w1Tb = []
 
-        def prep_w1():
+        def prep_w1(a):
             w1w = w1_sb[:].bitcast(F32).rearrange("p (a j r) -> p a j r", a=2, r=3)
-            for a in range(2):
-                bk = tp.tile([P, 3, P], F32, name="bk_w1", tag="tp")
-                for r in range(3):
-                    nc.tensor.transpose(bk[:, r, :], w1w[:, a, :, r], ident_f[:])
-                wt = keep.tile([P, 3 * P], F32, name="w1T%d" % a)
-                evac("sv"[a], wt[:].rearrange("p (r o) -> p r o", r=3), bk[:])
-                w1Tb.append(wt[:].bitcast(BF16).rearrange("p (r o e) -> p r o e", r=3, e=2))
+            bk = tp.tile([P, 3, P], F32, name="bk_w1", tag="tp")
+            for r in range(3):
+                nc.tensor.transpose(bk[:, r, :], w1w[:, a, :, r], ident_f[:])
+            wt = keep.tile([P, 3 * P], F32, name="w1T%d" % a)
+            evac("s", wt[:].rearrange("p (r o) -> p r o", r=3), bk[:])
+            w1Tb.append(wt[:].bitcast(BF16).rearrange("p (r o e) -> p r o e", r=3, e=2))
 
         gw = keep.tile([P, 2048], BF16, name="gw", align_bytes=64)
         wq = keep.tile([P, 512], U32, name="wq", align_bytes=64)
@@ -181,7 +180,7 @@ def tile_linearlayer_kernel(tc, x0e, x1o, x2e, w0e, w1o, w2e, bias, out):
             for r in range(3):
                 nc.tensor.transpose(bk1[:, r, :], xw[:, k, :, r], ident_f[:])
             xt = keep.tile([P, 3 * P], F32, name="x1T%d" % t)
-            evac("s", xt[:].rearrange("p (r n) -> p r n", r=3), bk1[:])
+            evac("v" if t < 2 else "s", xt[:].rearrange("p (r n) -> p r n", r=3), bk1[:])
             x1Tb[t] = xt[:].bitcast(BF16).rearrange("p (r n e) -> p r n e", r=3, e=2)
 
         def flip2(t):
@@ -239,39 +238,48 @@ def tile_linearlayer_kernel(tc, x0e, x1o, x2e, w0e, w1o, w2e, bias, out):
             eng = "v" if (t == NT - 1 and h == 0) else "s"
             evac(eng, o_sb[:, c0 : c0 + 320].rearrange("p (o m) -> p o m", m=5), py[:].rearrange("p m o -> p o m"))
 
+        def store(t, lo, hi):
+            nc.sync.dma_start(out=outv[:, t, lo:hi], in_=o_of(t)[:, lo:hi])
+
         sort_w2()
         for g in range(NT // 2):
             sort2(g)
 
-        prep_w1()
+        prep_w1(0)
         flip1(0)
+        prep_w1(1)
         flip1(1)
+        mm1(0, 0)
+        mm1(0, 1)
+        store(0, 512, 1280)
         prep_bias()
         prep_w0()
+        mm1(1, 0)
+        mm1(1, 1)
+        store(1, 512, 1280)
         flip0(0)
         quant_w0()
+        flip1(2)
         prep_w2()
         quant0(0)
         flip2(0)
         flip2(1)
         for t in range(NT):
-            nxt = t + 2
-            if nxt < NT:
-                flip1(nxt)
-            mm1(t, 0)
+            if t + 3 < NT:
+                flip1(t + 3)
+            if t + 2 < NT:
+                mm1(t + 2, 0)
             mm0(t)
-            mm1(t, 1)
-            if t == NT - 1:
-                nc.sync.dma_start(out=outv[:, t, 0:1280], in_=o_of(t)[:, 0:1280])
-            if nxt < NT and t % 2 == 0:
-                flip0(nxt // 2)
-            if nxt < NT:
-                flip2(nxt)
+            store(t, 0, 512)
+            if t + 2 < NT:
+                mm1(t + 2, 1)
+                store(t + 2, 512, 1280)
+            if t + 2 < NT and t % 2 == 0:
+                flip0((t + 2) // 2)
+            if t + 2 < NT:
+                flip2(t + 2)
             mm2(t, 0)
             mm2(t, 1)
-            if nxt < NT and t % 2 == 0:
-                quant0(nxt // 2)
-            if t == NT - 1:
-                nc.sync.dma_start(out=outv[:, t, 1280:1920], in_=o_of(t)[:, 1280:1920])
-            else:
-                nc.sync.dma_start(out=outv[:, t, :], in_=o_of(t)[:])
+            store(t, 1280, 1920)
+            if t + 2 < NT and t % 2 == 0:
+                quant0((t + 2) // 2)

@@ -70,20 +70,17 @@ def tile_linearlayer_kernel(tc, x0e, x1o, x2e, w0e, w1o, w2e, bias, out):
         load_x(1, 0)
         nc.sync.dma_start(out=brow[0:1, :], in_=bias.rearrange("(a o) -> a o", a=1))
         w0_sb = keep.tile([P, 4 * 512], BF16, name="w0_sb")
-        nc.sync.dma_start(
-            out=w0_sb[:].rearrange("p (a c) -> p a c", a=4),
-            in_=w0e.rearrange("(a p) i d -> p a (i d)", p=P),
-        )
+        nc.sync.dma_start(out=w0_sb[:], in_=w0e.rearrange("(p a) i d -> p (a i d)", a=4))
         load_x(0, 0)
+        load_x(1, 1)
         w2_sb = keep.tile([P, 640], BF16, name="w2_sb")
         nc.sync.dma_start(out=w2_sb[:], in_=w2e.rearrange("o i d -> o (i d)"))
-        load_x(2, 0)
-        load_x(1, 1)
-        load_x(2, 1)
         load_x(0, 1)
-        load_x(2, 2)
+        load_x(2, 0)
+        load_x(2, 1)
         load_x(1, 2)
         load_x(0, 2)
+        load_x(2, 2)
 
         bias_bc = keep.tile([P, 512], F32, name="bias_bc")
 
@@ -224,7 +221,12 @@ def tile_linearlayer_kernel(tc, x0e, x1o, x2e, w0e, w1o, w2e, bias, out):
                 rhs=wq[:].bitcast(FP8X4), rhs_scale=ws[:],
                 start=True, stop=True,
             )
-            nc.vector.tensor_tensor(out=o_sb[:, 0:512], in0=p0[:], in1=bias_bc[:], op=ADD)
+            nc.vector.tensor_tensor(
+                out=o_sb[:, 0:512].rearrange("p (q a) -> p q a", a=4),
+                in0=p0[:].rearrange("p (a q) -> p q a", a=4),
+                in1=bias_bc[:].rearrange("p (q a) -> p q a", a=4),
+                op=ADD,
+            )
 
         def mm2(t, h):
             o_sb = o_of(t)
@@ -251,35 +253,37 @@ def tile_linearlayer_kernel(tc, x0e, x1o, x2e, w0e, w1o, w2e, bias, out):
         flip1(1)
         mm1(0, 0)
         mm1(0, 1)
-        store(0, 512, 1280)
         prep_bias()
         prep_w0()
-        mm1(1, 0)
-        mm1(1, 1)
-        store(1, 512, 1280)
         flip0(0)
         quant_w0()
         flip1(2)
-        prep_w2()
         quant0(0)
+        prep_w2()
+        flip0(1)
+        mm1(1, 0)
+        mm0(0)
+        store(0, 0, 1280)
+        mm0(1)
+        mm1(1, 1)
+        store(1, 0, 1280)
+        quant0(1)
         flip2(0)
         flip2(1)
-        for t in range(NT):
-            if t + 3 < NT:
-                flip1(t + 3)
-            if t + 2 < NT:
-                mm1(t + 2, 0)
-            mm0(t)
-            store(t, 0, 512)
-            if t + 2 < NT:
-                mm1(t + 2, 1)
-                store(t + 2, 512, 1280)
-            if t + 2 < NT and t % 2 == 0:
-                flip0((t + 2) // 2)
-            if t + 2 < NT:
-                flip2(t + 2)
-            mm2(t, 0)
-            mm2(t, 1)
-            store(t, 1280, 1920)
-            if t + 2 < NT and t % 2 == 0:
-                quant0((t + 2) // 2)
+        for u in range(2, NT + 2):
+            if u + 1 < NT:
+                flip1(u + 1)
+            if u < NT:
+                mm1(u, 0)
+                mm0(u)
+                mm1(u, 1)
+                store(u, 0, 1280)
+            if u % 2 == 0 and u + 2 < NT:
+                flip0((u + 2) // 2)
+            if u < NT:
+                flip2(u)
+            mm2(u - 2, 0)
+            mm2(u - 2, 1)
+            store(u - 2, 1280, 1920)
+            if u % 2 == 0 and u + 2 < NT:
+                quant0((u + 2) // 2)

@@ -7,6 +7,7 @@ FLOPS = 2 * 1024 * (512 * 512 + 3 * 256 * 256 + 5 * 128 * 128)
 
 BF16 = mybir.dt.bfloat16
 F32 = mybir.dt.float32
+I32 = mybir.dt.int32
 U32 = mybir.dt.uint32
 U8 = mybir.dt.uint8
 FP8X4 = mybir.dt.float8_e4m3fn_x4
@@ -15,22 +16,29 @@ MULT = mybir.AluOpType.mult
 
 P = 128
 NT = 8
-MANUAL = True
-CHUNKS = ((0, 2), (2, 4), (4, 8))
+DUMMIES = 0
+LEAD = 3
+WIDTH = {0: 512, 1: 768, 2: 640}
+CHUNKS = {
+    0: ((0, 2), (2, 4), (4, 8)),
+    1: ((0, 1), (1, 2), (2, 4), (4, 8)),
+    2: ((0, 2), (2, 4), (4, 8)),
+}
 
 
 def tile_linearlayer_kernel(tc, x0e, x1o, x2e, w0e, w1o, w2e, bias, out):
     nc = tc.nc
     with ExitStack() as ctx:
-        if MANUAL:
-            ctx.enter_context(tc.manual_schedule())
+        ctx.enter_context(tc.manual_schedule())
         keep = ctx.enter_context(tc.tile_pool(name="keep", bufs=1))
         tp = ctx.enter_context(tc.psum_pool(name="tp", bufs=3))
         acc = ctx.enter_context(tc.psum_pool(name="acc", bufs=5))
 
-        x0v = x0e.rearrange("(p t) i d -> p t (i d)", t=NT)
-        x1v = x1o.rearrange("(p t) i d -> p t (i d)", t=NT)
-        x2v = x2e.rearrange("(p t) i d -> p t (i d)", t=NT)
+        xv = {
+            0: x0e.rearrange("(p t) i d -> p t (i d)", t=NT),
+            1: x1o.rearrange("(p t) i d -> p t (i d)", t=NT),
+            2: x2e.rearrange("(p t) i d -> p t (i d)", t=NT),
+        }
         outv = out.rearrange("(p t) c -> p t c", t=NT)
 
         def evac(eng, dst, src):
@@ -39,6 +47,17 @@ def tile_linearlayer_kernel(tc, x0e, x1o, x2e, w0e, w1o, w2e, bias, out):
             else:
                 nc.scalar.copy(out=dst, in_=src)
 
+        if DUMMIES:
+            zq = keep.tile([P, 512], U32, name="zq", align_bytes=64)
+            nc.vector.memset(zq[:].bitcast(I32), 0)
+            zs = keep.tile([P, 512], U8, name="zs", align_bytes=64)
+            nc.vector.memset(zs[:].bitcast(I32), 0)
+            for d in range(DUMMIES):
+                pd = acc.tile([P, 512], F32, name="pd", tag="acc")
+                nc.tensor.matmul_mx(
+                    out=pd[:], lhsT=zq[:, 0:P].bitcast(FP8X4), lhsT_scale=zs[:, 0:P],
+                    rhs=zq[:].bitcast(FP8X4), rhs_scale=zs[:], start=True, stop=True,
+                )
         ident_f = keep.tile([P, P], F32, name="ident_f")
         make_identity(nc, ident_f[:])
         ident_b = keep.tile([P, P], BF16, name="ident_b")
@@ -50,37 +69,45 @@ def tile_linearlayer_kernel(tc, x0e, x1o, x2e, w0e, w1o, w2e, bias, out):
 
         where = {}
         x_sb = {}
+        for kind in range(3):
+            for c, (lo, hi) in enumerate(CHUNKS[kind]):
+                for t in range(lo, hi):
+                    where[(kind, t)] = (c, t - lo, hi - lo)
 
         def load_x(kind, c):
-            view, width = {0: (x0v, 512), 1: (x1v, 768), 2: (x2v, 640)}[kind]
-            lo, hi = CHUNKS[c]
-            a = keep.tile([P, (hi - lo) * width], BF16, name="x%d_sb%d" % (kind, c))
-            nc.sync.dma_start(out=a[:].rearrange("p (t c) -> p t c", t=hi - lo), in_=view[:, lo:hi, :])
+            lo, hi = CHUNKS[kind][c]
+            a = keep.tile([P, (hi - lo) * WIDTH[kind]], BF16, name="x%d_sb%d" % (kind, c))
+            nc.sync.dma_start(out=a[:].rearrange("p (t c) -> p t c", t=hi - lo), in_=xv[kind][:, lo:hi, :])
             x_sb[(kind, c)] = a
 
-        for c, (lo, hi) in enumerate(CHUNKS):
-            for t in range(lo, hi):
-                where[t] = (c, t - lo, hi - lo)
+        w1v = w1o.rearrange("(a p) i d -> a p (i d)", p=P)
+        w1_sb = []
 
-        w1_sb = keep.tile([P, 2 * 768], BF16, name="w1_sb")
-        nc.sync.dma_start(
-            out=w1_sb[:].rearrange("p (a c) -> p a c", a=2),
-            in_=w1o.rearrange("(a p) i d -> p a (i d)", p=P),
-        )
+        def load_w1(a):
+            w = keep.tile([P, 768], BF16, name="w1_sb%d" % a)
+            nc.sync.dma_start(out=w[:], in_=w1v[a])
+            w1_sb.append(w)
+
+        load_w1(0)
         load_x(1, 0)
-        nc.sync.dma_start(out=brow[0:1, :], in_=bias.rearrange("(a o) -> a o", a=1))
-        w0_sb = keep.tile([P, 4 * 512], BF16, name="w0_sb")
-        nc.sync.dma_start(out=w0_sb[:], in_=w0e.rearrange("(p a) i d -> p (a i d)", a=4))
-        load_x(0, 0)
+        load_w1(1)
         load_x(1, 1)
+        nc.sync.dma_start(out=brow[0:1, :], in_=bias.rearrange("(a o) -> a o", a=1))
         w2_sb = keep.tile([P, 640], BF16, name="w2_sb")
         nc.sync.dma_start(out=w2_sb[:], in_=w2e.rearrange("o i d -> o (i d)"))
-        load_x(0, 1)
         load_x(2, 0)
-        load_x(2, 1)
         load_x(1, 2)
-        load_x(0, 2)
+        w0_sb = keep.tile([P, 4 * 512], BF16, name="w0_sb")
+        nc.sync.dma_start(
+            out=w0_sb[:].rearrange("p (a c) -> p a c", a=4),
+            in_=w0e.rearrange("(a p) i d -> p a (i d)", p=P),
+        )
+        load_x(0, 0)
+        load_x(2, 1)
+        load_x(1, 3)
+        load_x(0, 1)
         load_x(2, 2)
+        load_x(0, 2)
 
         bias_bc = keep.tile([P, 512], F32, name="bias_bc")
 
@@ -108,10 +135,10 @@ def tile_linearlayer_kernel(tc, x0e, x1o, x2e, w0e, w1o, w2e, bias, out):
         w1Tb = []
 
         def prep_w1(a):
-            w1w = w1_sb[:].bitcast(F32).rearrange("p (a j r) -> p a j r", a=2, r=3)
+            w1w = w1_sb[a][:].bitcast(F32).rearrange("p (j r) -> p j r", r=3)
             bk = tp.tile([P, 3, P], F32, name="bk_w1", tag="tp")
             for r in range(3):
-                nc.tensor.transpose(bk[:, r, :], w1w[:, a, :, r], ident_f[:])
+                nc.tensor.transpose(bk[:, r, :], w1w[:, :, r], ident_f[:])
             wt = keep.tile([P, 3 * P], F32, name="w1T%d" % a)
             evac("s", wt[:].rearrange("p (r o) -> p r o", r=3), bk[:])
             w1Tb.append(wt[:].bitcast(BF16).rearrange("p (r o e) -> p r o e", r=3, e=2))
@@ -120,16 +147,15 @@ def tile_linearlayer_kernel(tc, x0e, x1o, x2e, w0e, w1o, w2e, bias, out):
         wq = keep.tile([P, 512], U32, name="wq", align_bytes=64)
         ws = keep.tile([P, 512], U8, name="ws", align_bytes=64)
 
-        def prep_w0():
+        def prep_w0(b):
             w0f = w0_sb[:].bitcast(F32)
             gwf = gw[:].bitcast(F32).rearrange("p (o u) -> p o u", u=2)
-            for b in range(2):
-                bk = tp.tile([P, 2, 256], F32, name="bk_w0", tag="tp")
-                for aa in range(2):
-                    for u in range(2):
-                        c0 = 256 * (2 * b + aa) + 128 * u
-                        nc.tensor.transpose(bk[:, u, aa * P : (aa + 1) * P], w0f[:, c0 : c0 + P], ident_f[:])
-                evac("vs"[b], gwf[:, 256 * b : 256 * b + 256, :], bk[:].rearrange("p u o -> p o u"))
+            bk = tp.tile([P, 2, 256], F32, name="bk_w0", tag="tp")
+            for aa in range(2):
+                for u in range(2):
+                    c0 = 256 * (2 * b + aa) + 128 * u
+                    nc.tensor.transpose(bk[:, u, aa * P : (aa + 1) * P], w0f[:, c0 : c0 + P], ident_f[:])
+            evac("vs"[b], gwf[:, 256 * b : 256 * b + 256, :], bk[:].rearrange("p u o -> p o u"))
 
         def quant_w0():
             nc.vector.quantize_mx(out=wq[:].bitcast(FP8X4), scales=ws[:], in_=gw[:])
@@ -142,7 +168,7 @@ def tile_linearlayer_kernel(tc, x0e, x1o, x2e, w0e, w1o, w2e, bias, out):
         x2d = {}
 
         def sort2(g):
-            c, k, n = where[2 * g]
+            c, k, n = where[(2, 2 * g)]
             d = keep.tile([P, 2 * 640], BF16, name="x2d%d" % g)
             nc.gpsimd.tensor_scalar(
                 out=d[:].rearrange("p (t m i) -> p t m i", t=2, m=5),
@@ -152,7 +178,7 @@ def tile_linearlayer_kernel(tc, x0e, x1o, x2e, w0e, w1o, w2e, bias, out):
             x2d[g] = d
 
         def flip0(g):
-            c, k, n = where[2 * g]
+            c, k, n = where[(0, 2 * g)]
             xf = x_sb[(0, c)][:].bitcast(F32)
             bk0 = tp.tile([P, 2, 256], F32, name="bk_x0", tag="tp")
             for tt in range(2):
@@ -171,7 +197,7 @@ def tile_linearlayer_kernel(tc, x0e, x1o, x2e, w0e, w1o, w2e, bias, out):
             xs[g] = s
 
         def flip1(t):
-            c, k, n = where[t]
+            c, k, n = where[(1, t)]
             xw = x_sb[(1, c)][:].bitcast(F32).rearrange("p (t j r) -> p t j r", t=n, r=3)
             bk1 = tp.tile([P, 3, P], F32, name="bk_x1", tag="tp")
             for r in range(3):
@@ -197,6 +223,9 @@ def tile_linearlayer_kernel(tc, x0e, x1o, x2e, w0e, w1o, w2e, bias, out):
                 o_sbs[t] = keep.tile([P, 1920], F32, name="o_sb%d" % t)
             return o_sbs[t]
 
+        def store(t, lo, hi):
+            nc.sync.dma_start(out=outv[:, t, lo:hi], in_=o_of(t)[:, lo:hi])
+
         def mm1(t, h):
             o_sb = o_of(t)
             py = acc.tile([P, 3, P], F32, name="py1", tag="acc")
@@ -210,6 +239,8 @@ def tile_linearlayer_kernel(tc, x0e, x1o, x2e, w0e, w1o, w2e, bias, out):
             c0 = 512 + 384 * h
             eng = "s" if (h == 1 and t % 2 == 0) else "v"
             evac(eng, o_sb[:, c0 : c0 + 384].rearrange("p (o m) -> p o m", m=3), py[:].rearrange("p m o -> p o m"))
+            if h == 1:
+                store(t, 512, 1280)
 
         def mm0(t):
             o_sb = o_of(t)
@@ -221,15 +252,12 @@ def tile_linearlayer_kernel(tc, x0e, x1o, x2e, w0e, w1o, w2e, bias, out):
                 rhs=wq[:].bitcast(FP8X4), rhs_scale=ws[:],
                 start=True, stop=True,
             )
-            nc.vector.tensor_tensor(
-                out=o_sb[:, 0:512].rearrange("p (q a) -> p q a", a=4),
-                in0=p0[:].rearrange("p (a q) -> p q a", a=4),
-                in1=bias_bc[:].rearrange("p (q a) -> p q a", a=4),
-                op=ADD,
-            )
+            nc.vector.tensor_tensor(out=o_sb[:, 0:512], in0=p0[:], in1=bias_bc[:], op=ADD)
+            store(t, 0, 512)
 
         def mm2(t, h):
             o_sb = o_of(t)
+            last = t == NT - 1
             py = acc.tile([P, 5, 64], F32, name="py2", tag="acc")
             for m in range(5):
                 nc.tensor.matmul(
@@ -237,11 +265,12 @@ def tile_linearlayer_kernel(tc, x0e, x1o, x2e, w0e, w1o, w2e, bias, out):
                     start=True, stop=True,
                 )
             c0 = 1280 + 320 * h
-            eng = "v" if (t == NT - 1 and h == 0) else "s"
+            eng = "v" if (last and h == 0) else "s"
             evac(eng, o_sb[:, c0 : c0 + 320].rearrange("p (o m) -> p o m", m=5), py[:].rearrange("p m o -> p o m"))
-
-        def store(t, lo, hi):
-            nc.sync.dma_start(out=outv[:, t, lo:hi], in_=o_of(t)[:, lo:hi])
+            if last:
+                store(t, c0, c0 + 320)
+            elif h == 1:
+                store(t, 1280, 1920)
 
         sort_w2()
         for g in range(NT // 2):
@@ -254,36 +283,33 @@ def tile_linearlayer_kernel(tc, x0e, x1o, x2e, w0e, w1o, w2e, bias, out):
         mm1(0, 0)
         mm1(0, 1)
         prep_bias()
-        prep_w0()
-        flip0(0)
-        quant_w0()
         flip1(2)
+        prep_w0(0)
+        mm1(1, 0)
+        mm1(1, 1)
+        prep_w0(1)
+        flip0(0)
+        flip1(3)
+        quant_w0()
+        mm1(2, 0)
+        mm1(2, 1)
         quant0(0)
         prep_w2()
-        flip0(1)
-        mm1(1, 0)
-        mm0(0)
-        store(0, 0, 1280)
-        mm0(1)
-        mm1(1, 1)
-        store(1, 0, 1280)
-        quant0(1)
         flip2(0)
         flip2(1)
-        for u in range(2, NT + 2):
-            if u + 1 < NT:
-                flip1(u + 1)
-            if u < NT:
-                mm1(u, 0)
-                mm0(u)
-                mm1(u, 1)
-                store(u, 0, 1280)
-            if u % 2 == 0 and u + 2 < NT:
-                flip0((u + 2) // 2)
-            if u < NT:
-                flip2(u)
-            mm2(u - 2, 0)
-            mm2(u - 2, 1)
-            store(u - 2, 1280, 1920)
-            if u % 2 == 0 and u + 2 < NT:
-                quant0((u + 2) // 2)
+        for t in range(NT):
+            if t + LEAD + 1 < NT:
+                flip1(t + LEAD + 1)
+            if t + LEAD < NT:
+                mm1(t + LEAD, 0)
+            mm0(t)
+            if t + LEAD < NT:
+                mm1(t + LEAD, 1)
+            if t + 2 < NT and t % 2 == 0:
+                flip0((t + 2) // 2)
+            if t + 2 < NT:
+                flip2(t + 2)
+            mm2(t, 0)
+            mm2(t, 1)
+            if t + 2 < NT and t % 2 == 0:
+                quant0((t + 2) // 2)

@@ -17,7 +17,7 @@ MULT = mybir.AluOpType.mult
 P = 128
 NT = 8
 DUMMIES = 0
-LEAD = 3
+LEAD = 2
 WIDTH = {0: 512, 1: 768, 2: 640}
 CHUNKS = {
     0: ((0, 2), (2, 4), (4, 8)),
@@ -283,33 +283,35 @@ def tile_linearlayer_kernel(tc, x0e, x1o, x2e, w0e, w1o, w2e, bias, out):
         mm1(0, 0)
         mm1(0, 1)
         prep_bias()
-        flip1(2)
         prep_w0(0)
+        prep_w0(1)
         mm1(1, 0)
         mm1(1, 1)
-        prep_w0(1)
-        flip0(0)
+        flip1(2)
         flip1(3)
+        flip0(0)
         quant_w0()
-        mm1(2, 0)
-        mm1(2, 1)
-        quant0(0)
         prep_w2()
+        quant0(0)
         flip2(0)
         flip2(1)
-        for t in range(NT):
-            if t + LEAD + 1 < NT:
-                flip1(t + LEAD + 1)
-            if t + LEAD < NT:
-                mm1(t + LEAD, 0)
-            mm0(t)
-            if t + LEAD < NT:
-                mm1(t + LEAD, 1)
-            if t + 2 < NT and t % 2 == 0:
-                flip0((t + 2) // 2)
-            if t + 2 < NT:
-                flip2(t + 2)
-            mm2(t, 0)
-            mm2(t, 1)
-            if t + 2 < NT and t % 2 == 0:
-                quant0((t + 2) // 2)
+        for g in range(NT // 2):
+            a = 2 * g
+            for t in (a, a + 1):
+                if t + 2 < NT:
+                    mm1(t + 2, 0)
+                mm0(t)
+                if t + 2 < NT:
+                    mm1(t + 2, 1)
+            if a + 4 < NT:
+                flip1(a + 4)
+                flip1(a + 5)
+            if a + 2 < NT:
+                flip0(g + 1)
+            for t in (a, a + 1):
+                mm2(t, 0)
+                mm2(t, 1)
+            if a + 2 < NT:
+                quant0(g + 1)
+                flip2(a + 2)
+                flip2(a + 3)

@@ -18,6 +18,7 @@ P = 128
 NT = 8
 DUMMIES = 0
 LEAD = 2
+ROW = 1920
 WIDTH = {0: 512, 1: 768, 2: 640}
 CHUNKS = {
     0: ((0, 2), (2, 4), (4, 8)),
@@ -39,7 +40,7 @@ def tile_linearlayer_kernel(tc, x0e, x1o, x2e, w0e, w1o, w2e, bias, out):
             1: x1o.rearrange("(p t) i d -> p t (i d)", t=NT),
             2: x2e.rearrange("(p t) i d -> p t (i d)", t=NT),
         }
-        outv = out.rearrange("(p t) c -> p t c", t=NT)
+        outf = out.rearrange("(p t) c -> p (t c)", t=NT)
 
         def evac(eng, dst, src):
             if eng == "v":
@@ -216,15 +217,13 @@ def tile_linearlayer_kernel(tc, x0e, x1o, x2e, w0e, w1o, w2e, bias, out):
             evac("s", x2t[:], bk2[:])
             x2T[t] = x2t
 
-        o_sbs = {}
+        o_all = keep.tile([P, NT * ROW], F32, name="o_all")
 
         def o_of(t):
-            if t not in o_sbs:
-                o_sbs[t] = keep.tile([P, 1920], F32, name="o_sb%d" % t)
-            return o_sbs[t]
+            return o_all[:, ROW * t : ROW * (t + 1)]
 
-        def store(t, lo, hi):
-            nc.sync.dma_start(out=outv[:, t, lo:hi], in_=o_of(t)[:, lo:hi])
+        def store(lo, hi):
+            nc.sync.dma_start(out=outf[:, lo:hi], in_=o_all[:, lo:hi])
 
         def mm1(t, h):
             o_sb = o_of(t)
@@ -239,8 +238,6 @@ def tile_linearlayer_kernel(tc, x0e, x1o, x2e, w0e, w1o, w2e, bias, out):
             c0 = 512 + 384 * h
             eng = "s" if (h == 1 and t % 2 == 0) else "v"
             evac(eng, o_sb[:, c0 : c0 + 384].rearrange("p (o m) -> p o m", m=3), py[:].rearrange("p m o -> p o m"))
-            if h == 1:
-                store(t, 512, 1280)
 
         def mm0(t):
             o_sb = o_of(t)
@@ -253,7 +250,8 @@ def tile_linearlayer_kernel(tc, x0e, x1o, x2e, w0e, w1o, w2e, bias, out):
                 start=True, stop=True,
             )
             nc.vector.tensor_tensor(out=o_sb[:, 0:512], in0=p0[:], in1=bias_bc[:], op=ADD)
-            store(t, 0, 512)
+            if t % 2 == 0:
+                store(max(0, ROW * t - 640), ROW * t + 1280)
 
         def mm2(t, h):
             o_sb = o_of(t)
@@ -268,9 +266,9 @@ def tile_linearlayer_kernel(tc, x0e, x1o, x2e, w0e, w1o, w2e, bias, out):
             eng = "v" if (last and h == 0) else "s"
             evac(eng, o_sb[:, c0 : c0 + 320].rearrange("p (o m) -> p o m", m=5), py[:].rearrange("p m o -> p o m"))
             if last:
-                store(t, c0, c0 + 320)
-            elif h == 1:
-                store(t, 1280, 1920)
+                store(ROW * t + c0, ROW * t + c0 + 320)
+            elif h == 1 and t % 2 == 0:
+                store(ROW * t + 1280, ROW * (t + 1) + 1280)
 
         sort_w2()
         for g in range(NT // 2):

@@ -16,9 +16,6 @@ MULT = mybir.AluOpType.mult
 
 P = 128
 NT = 8
-DUMMIES = 0
-LEAD = 2
-ROW = 1920
 WIDTH = {0: 512, 1: 768, 2: 640}
 CHUNKS = {
     0: ((0, 2), (2, 4), (4, 8)),
@@ -40,7 +37,7 @@ def tile_linearlayer_kernel(tc, x0e, x1o, x2e, w0e, w1o, w2e, bias, out):
             1: x1o.rearrange("(p t) i d -> p t (i d)", t=NT),
             2: x2e.rearrange("(p t) i d -> p t (i d)", t=NT),
         }
-        outf = out.rearrange("(p t) c -> p (t c)", t=NT)
+        outv = out.rearrange("(p t) c -> p t c", t=NT)
 
         def evac(eng, dst, src):
             if eng == "v":
@@ -48,17 +45,6 @@ def tile_linearlayer_kernel(tc, x0e, x1o, x2e, w0e, w1o, w2e, bias, out):
             else:
                 nc.scalar.copy(out=dst, in_=src)
 
-        if DUMMIES:
-            zq = keep.tile([P, 512], U32, name="zq", align_bytes=64)
-            nc.vector.memset(zq[:].bitcast(I32), 0)
-            zs = keep.tile([P, 512], U8, name="zs", align_bytes=64)
-            nc.vector.memset(zs[:].bitcast(I32), 0)
-            for d in range(DUMMIES):
-                pd = acc.tile([P, 512], F32, name="pd", tag="acc")
-                nc.tensor.matmul_mx(
-                    out=pd[:], lhsT=zq[:, 0:P].bitcast(FP8X4), lhsT_scale=zs[:, 0:P],
-                    rhs=zq[:].bitcast(FP8X4), rhs_scale=zs[:], start=True, stop=True,
-                )
         ident_f = keep.tile([P, P], F32, name="ident_f")
         make_identity(nc, ident_f[:])
         ident_b = keep.tile([P, P], BF16, name="ident_b")
@@ -89,26 +75,36 @@ def tile_linearlayer_kernel(tc, x0e, x1o, x2e, w0e, w1o, w2e, bias, out):
             nc.sync.dma_start(out=w[:], in_=w1v[a])
             w1_sb.append(w)
 
-        load_w1(0)
+        w2_sb = keep.tile([P, 640], BF16, name="w2_sb")
+        w0_sb = keep.tile([P, 4 * 512], BF16, name="w0_sb")
+
+        def load_bias():
+            nc.sync.dma_start(out=brow[0:1, :], in_=bias.rearrange("(a o) -> a o", a=1))
+
+        def load_w2():
+            nc.sync.dma_start(out=w2_sb[:], in_=w2e.rearrange("o i d -> o (i d)"))
+
+        def load_w0():
+            nc.sync.dma_start(
+                out=w0_sb[:].rearrange("p (a c) -> p a c", a=4),
+                in_=w0e.rearrange("(a p) i d -> p a (i d)", p=P),
+            )
+
         load_x(1, 0)
+        load_w1(0)
         load_w1(1)
         load_x(1, 1)
-        nc.sync.dma_start(out=brow[0:1, :], in_=bias.rearrange("(a o) -> a o", a=1))
-        w2_sb = keep.tile([P, 640], BF16, name="w2_sb")
-        nc.sync.dma_start(out=w2_sb[:], in_=w2e.rearrange("o i d -> o (i d)"))
+        load_x(0, 0)
+        load_bias()
+        load_w2()
+        load_w0()
         load_x(2, 0)
         load_x(1, 2)
-        w0_sb = keep.tile([P, 4 * 512], BF16, name="w0_sb")
-        nc.sync.dma_start(
-            out=w0_sb[:].rearrange("p (a c) -> p a c", a=4),
-            in_=w0e.rearrange("(a p) i d -> p a (i d)", p=P),
-        )
-        load_x(0, 0)
-        load_x(2, 1)
-        load_x(1, 3)
         load_x(0, 1)
-        load_x(2, 2)
         load_x(0, 2)
+        load_x(2, 1)
+        load_x(2, 2)
+        load_x(1, 3)
 
         bias_bc = keep.tile([P, 512], F32, name="bias_bc")
 
@@ -197,35 +193,37 @@ def tile_linearlayer_kernel(tc, x0e, x1o, x2e, w0e, w1o, w2e, bias, out):
             xq[g] = q
             xs[g] = s
 
-        def flip1(t):
+        def flip1(t, eng):
             c, k, n = where[(1, t)]
             xw = x_sb[(1, c)][:].bitcast(F32).rearrange("p (t j r) -> p t j r", t=n, r=3)
             bk1 = tp.tile([P, 3, P], F32, name="bk_x1", tag="tp")
             for r in range(3):
                 nc.tensor.transpose(bk1[:, r, :], xw[:, k, :, r], ident_f[:])
             xt = keep.tile([P, 3 * P], F32, name="x1T%d" % t)
-            evac("v" if t < 2 else "s", xt[:].rearrange("p (r n) -> p r n", r=3), bk1[:])
+            evac(eng, xt[:].rearrange("p (r n) -> p r n", r=3), bk1[:])
             x1Tb[t] = xt[:].bitcast(BF16).rearrange("p (r n e) -> p r n e", r=3, e=2)
 
-        def flip2(t):
+        def flip2(t, eng):
             g, tt = divmod(t, 2)
             bk2 = tp.tile([P, 5, P], BF16, name="bk_x2", tag="tp")
             for m in range(5):
                 c0 = 640 * tt + 128 * m
                 nc.tensor.transpose(bk2[:, m, :], x2d[g][:, c0 : c0 + P], ident_b[:])
             x2t = keep.tile([P, 5, P], BF16, name="x2T%d" % t)
-            evac("s", x2t[:], bk2[:])
+            evac(eng, x2t[:], bk2[:])
             x2T[t] = x2t
 
-        o_all = keep.tile([P, NT * ROW], F32, name="o_all")
+        o_sbs = {}
 
         def o_of(t):
-            return o_all[:, ROW * t : ROW * (t + 1)]
+            if t not in o_sbs:
+                o_sbs[t] = keep.tile([P, 1920], F32, name="o_sb%d" % t)
+            return o_sbs[t]
 
-        def store(lo, hi):
-            nc.sync.dma_start(out=outf[:, lo:hi], in_=o_all[:, lo:hi])
+        def store(t, lo, hi):
+            nc.sync.dma_start(out=outv[:, t, lo:hi], in_=o_of(t)[:, lo:hi])
 
-        def mm1(t, h):
+        def mm1(t, h, eng):
             o_sb = o_of(t)
             py = acc.tile([P, 3, P], F32, name="py1", tag="acc")
             for m in range(3):
@@ -236,7 +234,6 @@ def tile_linearlayer_kernel(tc, x0e, x1o, x2e, w0e, w1o, w2e, bias, out):
                         start=(par == 0), stop=(par == 1),
                     )
             c0 = 512 + 384 * h
-            eng = "s" if (h == 1 and t % 2 == 0) else "v"
             evac(eng, o_sb[:, c0 : c0 + 384].rearrange("p (o m) -> p o m", m=3), py[:].rearrange("p m o -> p o m"))
 
         def mm0(t):
@@ -250,12 +247,9 @@ def tile_linearlayer_kernel(tc, x0e, x1o, x2e, w0e, w1o, w2e, bias, out):
                 start=True, stop=True,
             )
             nc.vector.tensor_tensor(out=o_sb[:, 0:512], in0=p0[:], in1=bias_bc[:], op=ADD)
-            if t % 2 == 0:
-                store(max(0, ROW * t - 640), ROW * t + 1280)
 
-        def mm2(t, h):
+        def mm2(t, h, eng):
             o_sb = o_of(t)
-            last = t == NT - 1
             py = acc.tile([P, 5, 64], F32, name="py2", tag="acc")
             for m in range(5):
                 nc.tensor.matmul(
@@ -263,53 +257,105 @@ def tile_linearlayer_kernel(tc, x0e, x1o, x2e, w0e, w1o, w2e, bias, out):
                     start=True, stop=True,
                 )
             c0 = 1280 + 320 * h
-            eng = "v" if (last and h == 0) else "s"
             evac(eng, o_sb[:, c0 : c0 + 320].rearrange("p (o m) -> p o m", m=5), py[:].rearrange("p m o -> p o m"))
-            if last:
-                store(ROW * t + c0, ROW * t + c0 + 320)
-            elif h == 1 and t % 2 == 0:
-                store(ROW * t + 1280, ROW * (t + 1) + 1280)
 
         sort_w2()
         for g in range(NT // 2):
             sort2(g)
 
+        flip1(0, "s")
         prep_w1(0)
-        flip1(0)
         prep_w1(1)
-        flip1(1)
-        mm1(0, 0)
-        mm1(0, 1)
-        prep_bias()
+        flip1(1, "v")
+        flip0(0)
+        mm1(0, 0, "s")
+        mm1(0, 1, "v")
+        store(0, 512, 1280)
+        mm1(1, 0, "v")
+        prep_w2()
         prep_w0(0)
         prep_w0(1)
-        mm1(1, 0)
-        mm1(1, 1)
-        flip1(2)
-        flip1(3)
-        flip0(0)
-        quant_w0()
-        prep_w2()
         quant0(0)
-        flip2(0)
-        flip2(1)
-        for g in range(NT // 2):
-            a = 2 * g
-            for t in (a, a + 1):
-                if t + 2 < NT:
-                    mm1(t + 2, 0)
-                mm0(t)
-                if t + 2 < NT:
-                    mm1(t + 2, 1)
-            if a + 4 < NT:
-                flip1(a + 4)
-                flip1(a + 5)
-            if a + 2 < NT:
-                flip0(g + 1)
-            for t in (a, a + 1):
-                mm2(t, 0)
-                mm2(t, 1)
-            if a + 2 < NT:
-                quant0(g + 1)
-                flip2(a + 2)
-                flip2(a + 3)
+        prep_bias()
+        flip1(2, "s")
+        flip2(0, "s")
+        mm1(1, 1, "s")
+        store(1, 512, 1280)
+        quant_w0()
+        flip0(1)
+        flip0(2)
+        flip2(1, "s")
+        mm1(2, 0, "v")
+        mm1(2, 1, "s")
+        store(2, 512, 1280)
+        quant0(1)
+        mm0(0)
+        store(0, 0, 512)
+        mm2(0, 0, "s")
+        mm0(1)
+        store(1, 0, 512)
+        mm2(0, 1, "v")
+        store(0, 1280, 1920)
+        flip2(2, "s")
+        flip2(3, "v")
+        flip0(3)
+        mm2(1, 0, "s")
+        mm2(1, 1, "s")
+        store(1, 1280, 1920)
+        mm0(2)
+        store(2, 0, 512)
+        mm2(2, 0, "s")
+        quant0(2)
+        mm2(2, 1, "v")
+        store(2, 1280, 1920)
+        flip1(3, "s")
+        flip1(4, "s")
+        flip2(4, "v")
+        mm2(3, 0, "s")
+        mm2(3, 1, "s")
+        store(3, 1280, 1920)
+        mm0(3)
+        store(3, 0, 512)
+        mm0(4)
+        store(4, 0, 512)
+        quant0(3)
+        mm1(3, 0, "s")
+        mm1(3, 1, "s")
+        store(3, 512, 1280)
+        mm1(4, 0, "v")
+        mm0(5)
+        store(5, 0, 512)
+        mm1(4, 1, "s")
+        store(4, 512, 1280)
+        mm2(4, 0, "s")
+        flip2(5, "v")
+        flip1(5, "s")
+        flip1(6, "s")
+        mm2(4, 1, "v")
+        store(4, 1280, 1920)
+        mm2(5, 0, "s")
+        mm2(5, 1, "s")
+        store(5, 1280, 1920)
+        mm0(6)
+        store(6, 0, 512)
+        mm1(5, 0, "s")
+        mm0(7)
+        store(7, 0, 512)
+        mm1(5, 1, "s")
+        store(5, 512, 1280)
+        flip2(6, "v")
+        flip2(7, "v")
+        flip1(7, "v")
+        mm2(6, 0, "s")
+        mm2(6, 1, "v")
+        store(6, 1280, 1920)
+        mm2(7, 0, "v")
+        mm2(7, 1, "s")
+        store(7, 1280, 1920)
+        mm1(6, 0, "v")
+        mm1(6, 1, "v")
+        store(6, 512, 1280)
+        mm1(7, 0, "v")
+        store(7, 512, 896)
+        mm1(7, 1, "v")
+        store(7, 896, 1280)

@@ -16,6 +16,7 @@ MULT = mybir.AluOpType.mult
 
 P = 128
 NT = 8
+ROW = 1920
 WIDTH = {0: 512, 1: 768, 2: 640}
 CHUNKS = {
     0: ((0, 2), (2, 4), (4, 8)),
@@ -37,7 +38,7 @@ def tile_linearlayer_kernel(tc, x0e, x1o, x2e, w0e, w1o, w2e, bias, out):
             1: x1o.rearrange("(p t) i d -> p t (i d)", t=NT),
             2: x2e.rearrange("(p t) i d -> p t (i d)", t=NT),
         }
-        outv = out.rearrange("(p t) c -> p t c", t=NT)
+        outf = out.rearrange("(p t) c -> p (t c)", t=NT)
 
         def evac(eng, dst, src):
             if eng == "v":
@@ -68,12 +69,12 @@ def tile_linearlayer_kernel(tc, x0e, x1o, x2e, w0e, w1o, w2e, bias, out):
             x_sb[(kind, c)] = a
 
         w1v = w1o.rearrange("(a p) i d -> a p (i d)", p=P)
-        w1_sb = []
+        w1_sb = {}
 
         def load_w1(a):
             w = keep.tile([P, 768], BF16, name="w1_sb%d" % a)
             nc.sync.dma_start(out=w[:], in_=w1v[a])
-            w1_sb.append(w)
+            w1_sb[a] = w
 
         w2_sb = keep.tile([P, 640], BF16, name="w2_sb")
         w0_sb = keep.tile([P, 4 * 512], BF16, name="w0_sb")
@@ -85,10 +86,7 @@ def tile_linearlayer_kernel(tc, x0e, x1o, x2e, w0e, w1o, w2e, bias, out):
             nc.sync.dma_start(out=w2_sb[:], in_=w2e.rearrange("o i d -> o (i d)"))
 
         def load_w0():
-            nc.sync.dma_start(
-                out=w0_sb[:].rearrange("p (a c) -> p a c", a=4),
-                in_=w0e.rearrange("(a p) i d -> p a (i d)", p=P),
-            )
+            nc.sync.dma_start(out=w0_sb[:], in_=w0e.rearrange("(p a) i d -> p (a i d)", a=4))
 
         load_x(1, 0)
         load_w1(0)
@@ -129,7 +127,7 @@ def tile_linearlayer_kernel(tc, x0e, x1o, x2e, w0e, w1o, w2e, bias, out):
                 nc.tensor.transpose(bk[:, m, :], w2d[:, m * P : (m + 1) * P], ident_b[:])
             evac("s", w2T[:], bk[:])
 
-        w1Tb = []
+        w1Tb = {}
 
         def prep_w1(a):
             w1w = w1_sb[a][:].bitcast(F32).rearrange("p (j r) -> p j r", r=3)
@@ -138,7 +136,7 @@ def tile_linearlayer_kernel(tc, x0e, x1o, x2e, w0e, w1o, w2e, bias, out):
                 nc.tensor.transpose(bk[:, r, :], w1w[:, :, r], ident_f[:])
             wt = keep.tile([P, 3 * P], F32, name="w1T%d" % a)
             evac("s", wt[:].rearrange("p (r o) -> p r o", r=3), bk[:])
-            w1Tb.append(wt[:].bitcast(BF16).rearrange("p (r o e) -> p r o e", r=3, e=2))
+            w1Tb[a] = wt[:].bitcast(BF16).rearrange("p (r o e) -> p r o e", r=3, e=2)
 
         gw = keep.tile([P, 2048], BF16, name="gw", align_bytes=64)
         wq = keep.tile([P, 512], U32, name="wq", align_bytes=64)
@@ -146,13 +144,13 @@ def tile_linearlayer_kernel(tc, x0e, x1o, x2e, w0e, w1o, w2e, bias, out):
 
         def prep_w0(b):
             w0f = w0_sb[:].bitcast(F32)
-            gwf = gw[:].bitcast(F32).rearrange("p (o u) -> p o u", u=2)
+            gwf = gw[:].bitcast(F32).rearrange("p (q a u) -> p q a u", a=4, u=2)
             bk = tp.tile([P, 2, 256], F32, name="bk_w0", tag="tp")
             for aa in range(2):
                 for u in range(2):
                     c0 = 256 * (2 * b + aa) + 128 * u
                     nc.tensor.transpose(bk[:, u, aa * P : (aa + 1) * P], w0f[:, c0 : c0 + P], ident_f[:])
-            evac("vs"[b], gwf[:, 256 * b : 256 * b + 256, :], bk[:].rearrange("p u o -> p o u"))
+            evac("v", gwf[:, :, 2 * b : 2 * b + 2, :], bk[:].rearrange("p u (aa q) -> p q aa u", aa=2))
 
         def quant_w0():
             nc.vector.quantize_mx(out=wq[:].bitcast(FP8X4), scales=ws[:], in_=gw[:])
@@ -193,12 +191,29 @@ def tile_linearlayer_kernel(tc, x0e, x1o, x2e, w0e, w1o, w2e, bias, out):
             xq[g] = q
             xs[g] = s
 
-        def flip1(t, eng):
+        x1d = {}
+
+        def sort1(t):
             c, k, n = where[(1, t)]
-            xw = x_sb[(1, c)][:].bitcast(F32).rearrange("p (t j r) -> p t j r", t=n, r=3)
+            d = keep.tile([P, 768], BF16, name="x1d%d" % t)
+            nc.gpsimd.tensor_scalar(
+                out=d[:].rearrange("p (r j e) -> p r j e", r=3, e=2),
+                in0=x_sb[(1, c)][:, 768 * k : 768 * (k + 1)].rearrange("p (j r e) -> p r j e", r=3, e=2),
+                scalar1=1.0, scalar2=0.0, op0=MULT, op1=ADD,
+            )
+            x1d[t] = d
+
+        def flip1(t, eng):
             bk1 = tp.tile([P, 3, P], F32, name="bk_x1", tag="tp")
-            for r in range(3):
-                nc.tensor.transpose(bk1[:, r, :], xw[:, k, :, r], ident_f[:])
+            if t in x1d:
+                xs_w = x1d[t][:].bitcast(F32)
+                for r in range(3):
+                    nc.tensor.transpose(bk1[:, r, :], xs_w[:, r * P : (r + 1) * P], ident_f[:])
+            else:
+                c, k, n = where[(1, t)]
+                xw = x_sb[(1, c)][:].bitcast(F32).rearrange("p (t j r) -> p t j r", t=n, r=3)
+                for r in range(3):
+                    nc.tensor.transpose(bk1[:, r, :], xw[:, k, :, r], ident_f[:])
             xt = keep.tile([P, 3 * P], F32, name="x1T%d" % t)
             evac(eng, xt[:].rearrange("p (r n) -> p r n", r=3), bk1[:])
             x1Tb[t] = xt[:].bitcast(BF16).rearrange("p (r n e) -> p r n e", r=3, e=2)
@@ -213,15 +228,13 @@ def tile_linearlayer_kernel(tc, x0e, x1o, x2e, w0e, w1o, w2e, bias, out):
             evac(eng, x2t[:], bk2[:])
             x2T[t] = x2t
 
-        o_sbs = {}
+        o_all = keep.tile([P, NT * ROW], F32, name="o_all")
 
         def o_of(t):
-            if t not in o_sbs:
-                o_sbs[t] = keep.tile([P, 1920], F32, name="o_sb%d" % t)
-            return o_sbs[t]
+            return o_all[:, ROW * t : ROW * (t + 1)]
 
-        def store(t, lo, hi):
-            nc.sync.dma_start(out=outv[:, t, lo:hi], in_=o_of(t)[:, lo:hi])
+        def store(lo, hi):
+            nc.sync.dma_start(out=outf[:, lo:hi], in_=o_all[:, lo:hi])
 
         def mm1(t, h, eng):
             o_sb = o_of(t)
@@ -260,8 +273,13 @@ def tile_linearlayer_kernel(tc, x0e, x1o, x2e, w0e, w1o, w2e, bias, out):
             evac(eng, o_sb[:, c0 : c0 + 320].rearrange("p (o m) -> p o m", m=5), py[:].rearrange("p m o -> p o m"))
 
         sort_w2()
-        for g in range(NT // 2):
-            sort2(g)
+        sort2(0)
+        sort2(1)
+        sort2(2)
+        sort2(3)
+        sort1(5)
+        sort1(6)
+        sort1(7)
 
         flip1(0, "s")
         prep_w1(0)
@@ -270,7 +288,7 @@ def tile_linearlayer_kernel(tc, x0e, x1o, x2e, w0e, w1o, w2e, bias, out):
         flip0(0)
         mm1(0, 0, "s")
         mm1(0, 1, "v")
-        store(0, 512, 1280)
+        store(512, 1280)
         mm1(1, 0, "v")
         prep_w2()
         prep_w0(0)
@@ -280,82 +298,75 @@ def tile_linearlayer_kernel(tc, x0e, x1o, x2e, w0e, w1o, w2e, bias, out):
         flip1(2, "s")
         flip2(0, "s")
         mm1(1, 1, "s")
-        store(1, 512, 1280)
+        store(2432, 3200)
         quant_w0()
         flip0(1)
         flip0(2)
         flip2(1, "s")
         mm1(2, 0, "v")
         mm1(2, 1, "s")
-        store(2, 512, 1280)
+        store(4352, 5120)
         quant0(1)
         mm0(0)
-        store(0, 0, 512)
+        store(0, 512)
         mm2(0, 0, "s")
         mm0(1)
-        store(1, 0, 512)
         mm2(0, 1, "v")
-        store(0, 1280, 1920)
+        store(1280, 2432)
         flip2(2, "s")
         flip2(3, "v")
         flip0(3)
         mm2(1, 0, "s")
         mm2(1, 1, "s")
-        store(1, 1280, 1920)
+        store(3200, 3840)
         mm0(2)
-        store(2, 0, 512)
+        store(3840, 4352)
         mm2(2, 0, "s")
         quant0(2)
         mm2(2, 1, "v")
-        store(2, 1280, 1920)
+        store(5120, 5760)
         flip1(3, "s")
         flip1(4, "s")
         flip2(4, "v")
         mm2(3, 0, "s")
         mm2(3, 1, "s")
-        store(3, 1280, 1920)
+        store(7040, 7680)
         mm0(3)
-        store(3, 0, 512)
         mm0(4)
-        store(4, 0, 512)
         quant0(3)
         mm1(3, 0, "s")
         mm1(3, 1, "s")
-        store(3, 512, 1280)
+        store(5760, 7040)
         mm1(4, 0, "v")
         mm0(5)
-        store(5, 0, 512)
         mm1(4, 1, "s")
-        store(4, 512, 1280)
+        store(7680, 8960)
         mm2(4, 0, "s")
         flip2(5, "v")
         flip1(5, "s")
         flip1(6, "s")
         mm2(4, 1, "v")
-        store(4, 1280, 1920)
+        store(8960, 10112)
         mm2(5, 0, "s")
         mm2(5, 1, "s")
-        store(5, 1280, 1920)
         mm0(6)
-        store(6, 0, 512)
+        store(10880, 12032)
         mm1(5, 0, "s")
         mm0(7)
-        store(7, 0, 512)
         mm1(5, 1, "s")
-        store(5, 512, 1280)
+        store(10112, 10880)
         flip2(6, "v")
         flip2(7, "v")
         flip1(7, "v")
         mm2(6, 0, "s")
         mm2(6, 1, "v")
-        store(6, 1280, 1920)
+        store(12800, 13440)
         mm2(7, 0, "v")
         mm2(7, 1, "s")
-        store(7, 1280, 1920)
+        store(14720, 15360)
         mm1(6, 0, "v")
         mm1(6, 1, "v")
-        store(6, 512, 1280)
+        store(12032, 12800)
         mm1(7, 0, "v")
-        store(7, 512, 896)
         mm1(7, 1, "v")
-        store(7, 896, 1280)
+        store(13440, 14720)

from contextlib import ExitStack

import concourse.mybir as mybir
from concourse.masks import make_identity

FLOPS = 2 * 1024 * (512 * 512 + 3 * 256 * 256 + 5 * 128 * 128)

BF16 = mybir.dt.bfloat16
F32 = mybir.dt.float32
I32 = mybir.dt.int32
U32 = mybir.dt.uint32
U8 = mybir.dt.uint8
FP8X4 = mybir.dt.float8_e4m3fn_x4
ADD = mybir.AluOpType.add
MULT = mybir.AluOpType.mult

P = 128
NT = 8
ROW = 1920
WIDTH = {0: 512, 1: 768, 2: 640}
CHUNKS = {
    0: ((0, 2), (2, 4), (4, 8)),
    1: ((0, 1), (1, 2), (2, 4), (4, 8)),
    2: ((0, 2), (2, 4), (4, 8)),
}


def tile_linearlayer_kernel(tc, x0e, x1o, x2e, w0e, w1o, w2e, bias, out):
    nc = tc.nc
    with ExitStack() as ctx:
        ctx.enter_context(tc.manual_schedule())
        keep = ctx.enter_context(tc.tile_pool(name="keep", bufs=1))
        tp = ctx.enter_context(tc.psum_pool(name="tp", bufs=3))
        acc = ctx.enter_context(tc.psum_pool(name="acc", bufs=5))

        xv = {
            0: x0e.rearrange("(p t) i d -> p t (i d)", t=NT),
            1: x1o.rearrange("(p t) i d -> p t (i d)", t=NT),
            2: x2e.rearrange("(p t) i d -> p t (i d)", t=NT),
        }
        outf = out.rearrange("(p t) c -> p (t c)", t=NT)

        def evac(eng, dst, src):
            if eng == "v":
                nc.vector.tensor_copy(out=dst, in_=src)
            else:
                nc.scalar.copy(out=dst, in_=src)

        ident_f = keep.tile([P, P], F32, name="ident_f")
        make_identity(nc, ident_f[:])
        ident_b = keep.tile([P, P], BF16, name="ident_b")
        make_identity(nc, ident_b[:])
        ones = keep.tile([P, P], BF16, name="ones")
        nc.vector.memset(ones[:], 1.0)
        brow = keep.tile([P, 512], BF16, name="brow")
        nc.vector.memset(brow[:], 0.0)

        where = {}
        x_sb = {}
        for kind in range(3):
            for c, (lo, hi) in enumerate(CHUNKS[kind]):
                for t in range(lo, hi):
                    where[(kind, t)] = (c, t - lo, hi - lo)

        def load_x(kind, c):
            lo, hi = CHUNKS[kind][c]
            a = keep.tile([P, (hi - lo) * WIDTH[kind]], BF16, name="x%d_sb%d" % (kind, c))
            nc.sync.dma_start(out=a[:].rearrange("p (t c) -> p t c", t=hi - lo), in_=xv[kind][:, lo:hi, :])
            x_sb[(kind, c)] = a

        w1v = w1o.rearrange("(a p) i d -> a p (i d)", p=P)
        w1_sb = {}

        def load_w1(a):
            w = keep.tile([P, 768], BF16, name="w1_sb%d" % a)
            nc.sync.dma_start(out=w[:], in_=w1v[a])
            w1_sb[a] = w

        w2_sb = keep.tile([P, 640], BF16, name="w2_sb")
        w0_sb = keep.tile([P, 4 * 512], BF16, name="w0_sb")

        def load_bias():
            nc.sync.dma_start(out=brow[0:1, :], in_=bias.rearrange("(a o) -> a o", a=1))

        def load_w2():
            nc.sync.dma_start(out=w2_sb[:], in_=w2e.rearrange("o i d -> o (i d)"))

        def load_w0():
            nc.sync.dma_start(out=w0_sb[:], in_=w0e.rearrange("(p a) i d -> p (a i d)", a=4))

        load_x(1, 0)
        load_w1(0)
        load_w1(1)
        load_x(1, 1)
        load_x(0, 0)
        load_bias()
        load_w2()
        load_w0()
        load_x(2, 0)
        load_x(1, 2)
        load_x(0, 1)
        load_x(0, 2)
        load_x(2, 1)
        load_x(2, 2)
        load_x(1, 3)

        bias_bc = keep.tile([P, 512], F32, name="bias_bc")

        def prep_bias():
            pb = acc.tile([P, 512], F32, name="pb", tag="acc")
            nc.tensor.matmul(out=pb[:], lhsT=ones[:], rhs=brow[:], start=True, stop=True)
            evac("v", bias_bc[:], pb[:])

        w2d = keep.tile([P, 640], BF16, name="w2d")
        w2T = keep.tile([P, 5, P], BF16, name="w2T")

        def sort_w2():
            nc.gpsimd.tensor_scalar(
                out=w2d[:].rearrange("p (m i) -> p m i", m=5),
                in0=w2_sb[:].rearrange("p (i m) -> p m i", m=5),
                scalar1=1.0, scalar2=0.0, op0=MULT, op1=ADD,
            )

        def prep_w2():
            bk = tp.tile([P, 5, P], BF16, name="bk_w2", tag="tp")
            for m in range(5):
                nc.tensor.transpose(bk[:, m, :], w2d[:, m * P : (m + 1) * P], ident_b[:])
            evac("s", w2T[:], bk[:])

        w1Tb = {}

        def prep_w1(a):
            w1w = w1_sb[a][:].bitcast(F32).rearrange("p (j r) -> p j r", r=3)
            bk = tp.tile([P, 3, P], F32, name="bk_w1", tag="tp")
            for r in range(3):
                nc.tensor.transpose(bk[:, r, :], w1w[:, :, r], ident_f[:])
            wt = keep.tile([P, 3 * P], F32, name="w1T%d" % a)
            evac("s", wt[:].rearrange("p (r o) -> p r o", r=3), bk[:])
            w1Tb[a] = wt[:].bitcast(BF16).rearrange("p (r o e) -> p r o e", r=3, e=2)

        gw = keep.tile([P, 2048], BF16, name="gw", align_bytes=64)
        wq = keep.tile([P, 512], U32, name="wq", align_bytes=64)
        ws = keep.tile([P, 512], U8, name="ws", align_bytes=64)

        def prep_w0(b):
            w0f = w0_sb[:].bitcast(F32)
            gwf = gw[:].bitcast(F32).rearrange("p (q a u) -> p q a u", a=4, u=2)
            bk = tp.tile([P, 2, 256], F32, name="bk_w0", tag="tp")
            for aa in range(2):
                for u in range(2):
                    c0 = 256 * (2 * b + aa) + 128 * u
                    nc.tensor.transpose(bk[:, u, aa * P : (aa + 1) * P], w0f[:, c0 : c0 + P], ident_f[:])
            evac("v", gwf[:, :, 2 * b : 2 * b + 2, :], bk[:].rearrange("p u (aa q) -> p q aa u", aa=2))

        def quant_w0():
            nc.vector.quantize_mx(out=wq[:].bitcast(FP8X4), scales=ws[:], in_=gw[:])

        gx = {}
        xq = {}
        xs = {}
        x1Tb = {}
        x2T = {}
        x2d = {}

        def sort2(g):
            c, k, n = where[(2, 2 * g)]
            d = keep.tile([P, 2 * 640], BF16, name="x2d%d" % g)
            nc.gpsimd.tensor_scalar(
                out=d[:].rearrange("p (t m i) -> p t m i", t=2, m=5),
                in0=x_sb[(2, c)][:, 640 * k : 640 * (k + 2)].rearrange("p (t i m) -> p t m i", t=2, m=5),
                scalar1=1.0, scalar2=0.0, op0=MULT, op1=ADD,
            )
            x2d[g] = d

        def flip0(g):
            c, k, n = where[(0, 2 * g)]
            xf = x_sb[(0, c)][:].bitcast(F32)
            bk0 = tp.tile([P, 2, 256], F32, name="bk_x0", tag="tp")
            for tt in range(2):
                for u in range(2):
                    c0 = 256 * (k + tt) + 128 * u
                    nc.tensor.transpose(bk0[:, u, tt * P : (tt + 1) * P], xf[:, c0 : c0 + P], ident_f[:])
            a = keep.tile([P, 1024], BF16, name="gx%d" % g, align_bytes=64)
            evac("v", a[:].bitcast(F32).rearrange("p (n u) -> p n u", u=2), bk0[:].rearrange("p u n -> p n u"))
            gx[g] = a

        def quant0(g):
            q = keep.tile([P, 256], U32, name="xq%d" % g, align_bytes=64)
            s = keep.tile([P, 256], U8, name="xs%d" % g, align_bytes=64)
            nc.vector.quantize_mx(out=q[:].bitcast(FP8X4), scales=s[:], in_=gx[g][:])
            xq[g] = q
            xs[g] = s

        x1d = {}

        def sort1(t):
            c, k, n = where[(1, t)]
            d = keep.tile([P, 768], BF16, name="x1d%d" % t)
            nc.gpsimd.tensor_scalar(
                out=d[:].rearrange("p (r j e) -> p r j e", r=3, e=2),
                in0=x_sb[(1, c)][:, 768 * k : 768 * (k + 1)].rearrange("p (j r e) -> p r j e", r=3, e=2),
                scalar1=1.0, scalar2=0.0, op0=MULT, op1=ADD,
            )
            x1d[t] = d

        def flip1(t, eng):
            bk1 = tp.tile([P, 3, P], F32, name="bk_x1", tag="tp")
            if t in x1d:
                xs_w = x1d[t][:].bitcast(F32)
                for r in range(3):
                    nc.tensor.transpose(bk1[:, r, :], xs_w[:, r * P : (r + 1) * P], ident_f[:])
            else:
                c, k, n = where[(1, t)]
                xw = x_sb[(1, c)][:].bitcast(F32).rearrange("p (t j r) -> p t j r", t=n, r=3)
                for r in range(3):
                    nc.tensor.transpose(bk1[:, r, :], xw[:, k, :, r], ident_f[:])
            xt = keep.tile([P, 3 * P], F32, name="x1T%d" % t)
            evac(eng, xt[:].rearrange("p (r n) -> p r n", r=3), bk1[:])
            x1Tb[t] = xt[:].bitcast(BF16).rearrange("p (r n e) -> p r n e", r=3, e=2)

        def flip2(t, eng):
            g, tt = divmod(t, 2)
            bk2 = tp.tile([P, 5, P], BF16, name="bk_x2", tag="tp")
            for m in range(5):
                c0 = 640 * tt + 128 * m
                nc.tensor.transpose(bk2[:, m, :], x2d[g][:, c0 : c0 + P], ident_b[:])
            x2t = keep.tile([P, 5, P], BF16, name="x2T%d" % t)
            evac(eng, x2t[:], bk2[:])
            x2T[t] = x2t

        o_all = keep.tile([P, NT * ROW], F32, name="o_all")

        def o_of(t):
            return o_all[:, ROW * t : ROW * (t + 1)]

        def store(lo, hi):
            nc.sync.dma_start(out=outf[:, lo:hi], in_=o_all[:, lo:hi])

        def mm1(t, h, eng):
            o_sb = o_of(t)
            py = acc.tile([P, 3, P], F32, name="py1", tag="acc")
            for m in range(3):
                for par in range(2):
                    r, e = divmod(3 * par + m, 2)
                    nc.tensor.matmul(
                        out=py[:, m, :], lhsT=x1Tb[t][:, r, :, e], rhs=w1Tb[h][:, r, :, e],
                        start=(par == 0), stop=(par == 1),
                    )
            c0 = 512 + 384 * h
            evac(eng, o_sb[:, c0 : c0 + 384].rearrange("p (o m) -> p o m", m=3), py[:].rearrange("p m o -> p o m"))

        def mm0(t):
            o_sb = o_of(t)
            g, tt = divmod(t, 2)
            p0 = acc.tile([P, 512], F32, name="p0", tag="acc")
            nc.tensor.matmul_mx(
                out=p0[:],
                lhsT=xq[g][:, tt * P : (tt + 1) * P].bitcast(FP8X4), lhsT_scale=xs[g][:, tt * P : (tt + 1) * P],
                rhs=wq[:].bitcast(FP8X4), rhs_scale=ws[:],
                start=True, stop=True,
            )
            nc.vector.tensor_tensor(out=o_sb[:, 0:512], in0=p0[:], in1=bias_bc[:], op=ADD)

        def mm2(t, h, eng):
            o_sb = o_of(t)
            py = acc.tile([P, 5, 64], F32, name="py2", tag="acc")
            for m in range(5):
                nc.tensor.matmul(
                    out=py[:, m, :], lhsT=x2T[t][:, m, :], rhs=w2T[:, m, 64 * h : 64 * h + 64],
                    start=True, stop=True,
                )
            c0 = 1280 + 320 * h
            evac(eng, o_sb[:, c0 : c0 + 320].rearrange("p (o m) -> p o m", m=5), py[:].rearrange("p m o -> p o m"))

        sort_w2()
        sort2(0)
        sort2(1)
        sort2(2)
        sort2(3)
        sort1(5)
        sort1(6)
        sort1(7)

        flip1(0, "s")
        prep_w1(0)
        prep_w1(1)
        flip1(1, "v")
        flip0(0)
        mm1(0, 0, "s")
        mm1(0, 1, "v")
        store(512, 1280)
        mm1(1, 0, "v")
        prep_w2()
        prep_w0(0)
        prep_w0(1)
        quant0(0)
        prep_bias()
        flip1(2, "s")
        flip2(0, "s")
        mm1(1, 1, "s")
        store(2432, 3200)
        quant_w0()
        flip0(1)
        flip0(2)
        flip2(1, "s")
        mm1(2, 0, "v")
        mm1(2, 1, "s")
        store(4352, 5120)
        quant0(1)
        mm0(0)
        store(0, 512)
        mm2(0, 0, "s")
        mm0(1)
        mm2(0, 1, "v")
        store(1280, 2432)
        flip2(2, "s")
        flip2(3, "v")
        flip0(3)
        mm2(1, 0, "s")
        mm2(1, 1, "s")
        store(3200, 3840)
        mm0(2)
        store(3840, 4352)
        mm2(2, 0, "s")
        quant0(2)
        mm2(2, 1, "v")
        store(5120, 5760)
        flip1(3, "s")
        flip1(4, "s")
        flip2(4, "v")
        mm2(3, 0, "s")
        mm2(3, 1, "s")
        store(7040, 7680)
        mm0(3)
        mm0(4)
        quant0(3)
        mm1(3, 0, "s")
        mm1(3, 1, "s")
        store(5760, 7040)
        mm1(4, 0, "v")
        mm0(5)
        mm1(4, 1, "s")
        store(7680, 8960)
        mm2(4, 0, "s")
        flip2(5, "v")
        flip1(5, "s")
        flip1(6, "s")
        mm2(4, 1, "v")
        store(8960, 10112)
        mm2(5, 0, "s")
        mm2(5, 1, "s")
        mm0(6)
        store(10880, 12032)
        mm1(5, 0, "s")
        mm0(7)
        mm1(5, 1, "s")
        store(10112, 10880)
        flip2(6, "v")
        flip2(7, "v")
        flip1(7, "v")
        mm2(6, 0, "s")
        mm2(6, 1, "v")
        store(12800, 13440)
        mm2(7, 0, "v")
        mm2(7, 1, "s")
        store(14720, 15360)
        mm1(6, 0, "v")
        mm1(6, 1, "v")
        store(12032, 12800)
        mm1(7, 0, "v")
        mm1(7, 1, "v")
        store(13440, 14720)
